import numpy as np
import ml_dtypes


def mxq(x, axis, fmt="e4m3"):
    dtype, down = {"e4m3": (ml_dtypes.float8_e4m3fn, 7), "e5m2": (ml_dtypes.float8_e5m2, 14)}[fmt]
    v = np.moveaxis(np.asarray(x, np.float32).astype(ml_dtypes.bfloat16).astype(np.float64), axis, -1)
    blocks = v.reshape(v.shape[:-1] + (-1, 32))
    amax = np.abs(blocks).max(-1, keepdims=True)
    byte = np.maximum(np.where(amax > 0, np.frexp(amax)[1] - 1 + 127, 0) - down, 1)
    scale = np.exp2(byte - 127.0)
    codes = (blocks / scale).astype(np.float32).astype(dtype).astype(np.float64)
    return np.moveaxis((codes * scale).reshape(v.shape), -1, axis)


WIDE = False


def mx_kscale(k):
    if not WIDE:
        return np.ones(k)
    levels = np.array([18, -18])
    if k % 512:
        return np.exp2(np.random.permutation(np.resize(levels, k // 32))).repeat(32)
    a = np.empty((k // 512, 16))
    for p in range(k // 512):
        a[p, :8] = np.random.permutation(np.resize(levels, 8))
        for g in range(8):
            far = levels[np.abs(levels - a[p, g]) >= 10]
            a[p, g + 8] = far[np.random.randint(len(far))]
    return np.exp2(a.ravel()).repeat(32)


BF16 = ml_dtypes.bfloat16


def bf(x):
    return np.asarray(x, np.float32).astype(BF16)


def f64(x):
    return np.asarray(x).astype(np.float64)


B, T, DM, DH = 2, 512, 1024, 1024
N = B * T


def sigmoid(x):
    return 1.0 / (1.0 + np.exp(-x))


def setup_inputs():
    s = mx_kscale(N).reshape(B, T, 1)
    u = mx_kscale(DM)
    v = mx_kscale(DH)
    q0 = bf(np.random.standard_normal((B, T, DM)))
    num = bf(np.random.standard_normal((B, T, DH)) * 1.9 * np.sqrt(T))
    den = bf(0.5 * T * (0.5 + np.random.random((B, T, DH))))
    Wq0 = bf(np.random.standard_normal((DH, DM)) / np.sqrt(DM))
    Wo0 = bf(np.random.standard_normal((DM, DH)) * 5.0 / np.sqrt(DH))
    g = bf(np.random.standard_normal((B, T, DM)) * 8.0 * np.exp2(np.random.randint(-6, 1, (B, T, 1))) / s * u)
    zq = f64(q0) @ f64(Wq0).T
    return {"q": bf(f64(q0) * s),
            "num": num,
            "den": den,
            "Wq": bf(f64(Wq0) / v[:, None]),
            "Wo": bf(f64(Wo0) * v / u[:, None]),
            "zq": np.asarray(zq, np.float32),
            "grad_out": g}


def reference(q, num, den, Wq, Wo, zq, grad_out):
    qf = f64(q).reshape(N, DM)
    gf = f64(grad_out).reshape(N, DM)
    ratio = f64(num).reshape(N, DH) / f64(den).reshape(N, DH)
    sg = sigmoid(f64(zq).reshape(N, DH))
    dy = mxq(gf, 1, "e5m2") @ mxq(f64(Wo), 0, "e4m3")
    dz = dy * ratio * (sg * (1.0 - sg))
    dq = mxq(dz, 1, "e5m2") @ mxq(f64(Wq), 0, "e4m3")
    dWq = mxq(dz, 0, "e5m2").T @ mxq(qf, 0, "e4m3")
    return dq.reshape(B, T, DM), dWq

@@ -1,0 +1,391 @@
+from contextlib import ExitStack
+
+import concourse.mybir as mybir
+from concourse.masks import make_identity
+
+F32 = mybir.dt.float32
+BF16 = mybir.dt.bfloat16
+U32 = mybir.dt.uint32
+U8 = mybir.dt.uint8
+E4M3 = mybir.dt.float8_e4m3fn_x4
+E5M2 = mybir.dt.float8_e5m2_x4
+ACT = mybir.ActivationFunctionType
+ALU = mybir.AluOpType
+
+P = 128
+PACK = 4
+PASS = P * PACK
+D = 1024
+FLOPS = 3 * 2 * D * D * D
+
+
+def tile_aftfull_pb_v_kernel(tc, q, num, den, Wq, Wo, zq, grad_out, out_0, out_1):
+    nc = tc.nc
+
+    def by_pass(x):
+        return x.rearrange("b t w -> (b t) w").rearrange("(g p j) w -> g p j w", g=2, j=PACK)
+
+    q_h, num_h, den_h, z_h, g_h, dq_h = (by_pass(x) for x in (q, num, den, zq, grad_out, out_0))
+    wq_h = Wq.rearrange("(g p j) w -> g p j w", g=2, j=PACK)
+    wo_h = Wo.rearrange("(g p j) w -> g p j w", g=2, j=PACK)
+
+    with ExitStack() as ctx:
+        sb = ctx.enter_context(tc.tile_pool(name="sb", bufs=1))
+        ps = ctx.enter_context(tc.psum_pool(name="ps", bufs=1))
+
+        def tiles(name, n, shape, dtype):
+            return [sb.tile(shape, dtype, name=name + str(i), align_bytes=64) for i in range(n)]
+
+        ident = sb.tile([P, P], F32, name="ident")
+        warm = sb.tile([P, 1], F32, name="warm")
+        den_sb = tiles("den", 4, [P, 2 * D], BF16)
+        grad_sb = tiles("grad", 4, [P, 2 * D], BF16)
+        num_sb = tiles("num", 4, [P, PACK, PASS], BF16)
+        z_sb = tiles("z", 4, [P, PACK, PASS], F32)
+        fac = tiles("fac", 2, [P, PACK, D], F32)
+        wo_raw = tiles("wo_raw", 4, [P, PACK, PASS], BF16)
+        rows = tiles("rows", 4, [P, PACK, PASS], BF16)
+        woven = tiles("woven", 3, [P, PASS * PACK], BF16)
+        turned = tiles("turned", 5, [P, 2 * PASS], BF16)
+        dz_sb = tiles("dz", 2, [P, PACK, PASS], BF16)
+
+        def operand(name, n, width):
+            return list(zip(tiles(name + "_codes", n, [P, width], U32), tiles(name + "_scales", n, [P, width], U8)))
+
+        wo_mx = operand("wo", 4, PASS)
+        q_mx = operand("q", 4, PASS)
+        wq_mx = operand("wq", 4, PASS)
+        gT_mx = operand("gT", 8, 2 * P)
+        dzT_mx = operand("dzT", 8, 2 * P)
+        dz_mx = operand("dz", 4, PASS)
+        banks = [ps.tile([P, PASS], F32, name="bank" + str(i)) for i in range(8)]
+        dy_banks, turn_banks, out_banks = banks[0:3], banks[3:5], banks[5:8]
+        staged = [t[:].bitcast(F32) for t in den_sb + grad_sb[0:2]]
+        count = {"woven": 0, "turned": 0, "dy": 0, "turn": 0, "out": 0, "staged": 0}
+
+        def take(kind, pool):
+            count[kind] = count[kind] + 1
+            return pool[(count[kind] - 1) % len(pool)]
+
+        def cols(c):
+            return slice(c * PASS, (c + 1) * PASS)
+
+        def load(dst, src):
+            nc.sync.dma_start(out=dst, in_=src)
+
+        def load_pair(dst, src, g, jj):
+            load(dst[2 * g + jj][:].rearrange("p (j w) -> p j w", j=2), src[g, :, 2 * jj : 2 * jj + 2, :])
+
+        def weave(src, copy=nc.vector.tensor_copy):
+            dst = take("woven", woven)[:, 0 : PACK * src.shape[2]]
+            copy(
+                out=dst.rearrange("p (c i t) -> p c t i", i=4, t=PACK),
+                in_=src.rearrange("p t (c i) -> p c t i", i=4),
+            )
+            return dst
+
+        def quantize(dst, src, fmt, lo=0):
+            hi = lo + src.shape[1] // PACK
+            nc.vector.quantize_mx(out=dst[0][:, lo:hi].bitcast(fmt), scales=dst[1][:, lo:hi], in_=src)
+
+        def prepare_two(dst_a, src_a, dst_b, src_b):
+            a, b = weave(src_a), weave(src_b)
+            quantize(dst_a, a, E4M3)
+            quantize(dst_b, b, E4M3)
+
+        def turn(halves, bank):
+            for h, words in enumerate(halves):
+                for u in range(2):
+                    nc.tensor.transpose(bank[:, (2 * h + u) * P : (2 * h + u + 1) * P], words[:, u : 2 * P : 2], ident[:])
+            return bank[:, 0 : 2 * P * len(halves)]
+
+        def turn_out(bank, copy=nc.scalar.copy):
+            dst = take("turned", turned)[:, 0 : 2 * bank.shape[1]]
+            copy(
+                out=dst.bitcast(F32).rearrange("p (h r u) -> p h r u", r=P, u=2),
+                in_=bank.rearrange("p (h u r) -> p h r u", r=P, u=2),
+            )
+            return dst
+
+        def turn_grad(g, j, bank):
+            words = grad_sb[2 * g + j // 2][:, (j % 2) * D : (j % 2 + 1) * D].bitcast(F32)
+            return turn([words[:, 0 : 2 * P], words[:, 2 * P : 4 * P]], bank)
+
+        def turn_dz(i, j0, n, bank):
+            return turn([dz_sb[i % 2][:, j, :].bitcast(F32) for j in range(j0, j0 + n)], bank)
+
+        def fac_part(i, jj):
+            return fac[i % 2][:, 2 * jj : 2 * jj + 2, cols(i // 2)]
+
+        def root_den(g, j0, n):
+            src = den_sb[2 * g + j0 // 2][:, (j0 % 2) * D : (j0 % 2 + n) * D]
+            nc.scalar.activation(out=fac[g][:, j0 : j0 + n, :].rearrange("p j w -> p (j w)"), in_=src, func=ACT.Abs_reciprocal_sqrt)
+
+        def square_root_den(i, jj):
+            nc.scalar.activation(out=fac_part(i, jj), in_=fac_part(i, jj), func=ACT.Square)
+
+        def times_num(i, jj):
+            nc.vector.tensor_tensor(out=fac_part(i, jj), in0=fac_part(i, jj), in1=num_sb[i][:, 2 * jj : 2 * jj + 2, :], op=ALU.mult)
+
+        def gate(i, jj, func):
+            part = z_sb[i][:, 2 * jj : 2 * jj + 2, :]
+            nc.scalar.activation(out=part, in_=part, func=func, scale=0.5 if func == ACT.Tanh else 1.0)
+
+        def times_gate(i, jj):
+            nc.vector.scalar_tensor_tensor(
+                out=fac_part(i, jj), in0=z_sb[i][:, 2 * jj : 2 * jj + 2, :], scalar=1.0, in1=fac_part(i, jj),
+                op0=ALU.subtract, op1=ALU.mult)
+
+        def product(bank, pairs, passes=(0, 1)):
+            for k in passes:
+                lhs, at, rhs = pairs[k]
+                nc.tensor.matmul_mx(
+                    out=bank[:], lhsT=lhs[0][:, at : at + P].bitcast(E5M2), lhsT_scale=lhs[1][:, at : at + P],
+                    rhs=rhs[0][:].bitcast(E4M3), rhs_scale=rhs[1][:], start=(k == 0), stop=(k == 1))
+
+        def dy(i, j, bank):
+            product(bank, [(gT_mx[4 * (i % 2) + j], k * P, wo_mx[2 * k + i // 2]) for k in range(2)])
+            return bank
+
+        def round_dz(i, j, bank, lo=0, hi=PASS):
+            nc.vector.scalar_tensor_tensor(
+                out=dz_sb[i % 2][:, j, lo:hi], in0=bank[:, lo:hi], scalar=-0.25,
+                in1=fac[i % 2][:, j, i // 2 * PASS + lo : i // 2 * PASS + hi], op0=ALU.mult, op1=ALU.mult)
+
+        def dq_pairs(g, j, n):
+            return [(dzT_mx[2 * (2 * c + g) + j // 2], (j % 2) * P, wq_mx[2 * c + n]) for c in range(2)]
+
+        def dw_pairs(c, m, n):
+            return [(dz_mx[2 * c + g], m * P, q_mx[2 * g + n]) for g in range(2)]
+
+        def dq_rows(g, j):
+            return dq_h[g, :, j, :]
+
+        def dw_rows(c, m):
+            return out_1[c * PASS + m * P : c * PASS + (m + 1) * P, :]
+
+        def begin(pairs_of, a, b, two):
+            for n in range(2):
+                product(two[n], pairs_of(a, b, n), (0,))
+
+        def emit(pairs_of, rows_of, a, b, two, copies, passes=(0, 1), split=False):
+            stage = take("staged", staged)
+            for n in range(2):
+                product(two[n], pairs_of(a, b, n), passes)
+                copies[n](out=stage[:, cols(n)], in_=two[n][:])
+                if split:
+                    nc.sync.dma_start(out=rows_of(a, b)[:, cols(n)], in_=stage[:, cols(n)])
+            if not split:
+                nc.sync.dma_start(out=rows_of(a, b), in_=stage)
+
+        def load_quarter(i):
+            load(num_sb[i][:], num_h[i % 2, :, :, cols(i // 2)])
+            load(z_sb[i][:], z_h[i % 2, :, :, cols(i // 2)])
+
+        def quantize_grad(g, jj, made):
+            for h in range(2):
+                quantize(gT_mx[4 * g + 2 * jj + h], made[h], E5M2)
+
+        on_scalar, on_vector = nc.scalar.copy, nc.vector.tensor_copy
+        SS, SV = (on_scalar, on_scalar), (on_scalar, on_vector)
+
+        def prepare(dst, src, copy=on_vector):
+            quantize(dst, weave(src, copy), E4M3)
+
+        def load_z(i, jj):
+            load(z_sb[i][:, 2 * jj : 2 * jj + 2, :], z_h[i % 2, :, 2 * jj : 2 * jj + 2, cols(i // 2)])
+
+        def load_num(i):
+            load(num_sb[i][:], num_h[i % 2, :, :, cols(i // 2)])
+
+        def load_rows(src, g, n):
+            load(rows[2 * g + n][:], src[g, :, :, cols(n)])
+
+        with tc.manual_schedule():
+            for j in range(2):
+                load(den_sb[0][:, j * D : (j + 1) * D], den_h[0, :, j, :])
+                load(wo_raw[2 * j][:], wo_h[j, :, :, cols(0)])
+            load_rows(q_h, 0, 0)
+            load_pair(den_sb, den_h, 0, 1)
+            load_rows(q_h, 0, 1)
+            load_pair(grad_sb, g_h, 0, 0)
+            load_pair(den_sb, den_h, 1, 0)
+            load_pair(grad_sb, g_h, 0, 1)
+            load_rows(q_h, 1, 0)
+            load_pair(den_sb, den_h, 1, 1)
+            load_rows(q_h, 1, 1)
+            load_z(0, 0)
+            load_num(0)
+            load_z(0, 1)
+            load_pair(grad_sb, g_h, 1, 0)
+            load_num(1)
+            load_pair(grad_sb, g_h, 1, 1)
+            load(z_sb[1][:], z_h[1, :, :, cols(0)])
+            for k in range(2):
+                load(wo_raw[2 * k + 1][:], wo_h[k, :, :, cols(1)])
+            load_num(2)
+            load(z_sb[2][:], z_h[0, :, :, cols(1)])
+
+            nc.vector.memset(warm[:], 1.0)
+            nc.scalar.activation(out=warm[:], in_=warm[:], func=ACT.Abs_reciprocal_sqrt)
+            make_identity(nc, ident[:])
+
+            root_den(0, 0, 1)
+            root_den(0, 1, 1)
+            square_root_den(0, 0)
+            square_root_den(2, 0)
+            root_den(0, 2, 2)
+            square_root_den(0, 1)
+            square_root_den(2, 1)
+            root_den(1, 0, 2)
+            root_den(1, 2, 2)
+            gate(0, 0, ACT.Tanh)
+            gate(0, 0, ACT.Square)
+            gate(0, 1, ACT.Tanh)
+            gate(0, 1, ACT.Square)
+
+            prepare(wo_mx[0], wo_raw[0][:])
+            prepare_two(wo_mx[2], wo_raw[2][:], q_mx[0], rows[0][:])
+            prepare(q_mx[1], rows[1][:])
+            for jj in range(2):
+                made = [turn_out(turn_grad(0, 2 * jj + h, banks[3 + 2 * jj + h]), on_vector) for h in range(2)]
+                quantize_grad(0, jj, made)
+            prepare_two(q_mx[2], rows[2][:], q_mx[3], rows[3][:])
+            load_rows(wq_h, 0, 0)
+            load_rows(wq_h, 0, 1)
+            load(z_sb[3][:], z_h[1, :, :, cols(1)])
+            load_num(3)
+            load_rows(wq_h, 1, 0)
+            load_rows(wq_h, 1, 1)
+            times_num(0, 0)
+            times_num(0, 1)
+
+            def outs():
+                return [take("out", out_banks), take("out", out_banks)]
+
+            held = [dy(0, j, banks[j]) for j in range(3)]
+            late = [turn_grad(1, j, banks[5 + j]) for j in range(2)]
+            times_gate(0, 0)
+            round_dz(0, 0, held[0])
+            round_dz(0, 1, held[1])
+            held.append(dy(0, 3, banks[0]))
+            first = turn_dz(0, 0, 2, banks[3])
+            times_gate(0, 1)
+            made = [turn_out(bank) for bank in late]
+            late = [turn_grad(1, 2, banks[7])]
+            round_dz(0, 2, held[2])
+            round_dz(0, 3, held[3])
+            second = turn_dz(0, 2, 2, banks[4])
+            late.append(turn_grad(1, 3, banks[5]))
+            quantize_grad(1, 0, made)
+            square_root_den(1, 0)
+            first = turn_out(first)
+            square_root_den(1, 1)
+            held = [dy(1, j, banks[1 + j]) for j in range(2)]
+            times_num(1, 0)
+            tokens = weave(dz_sb[0][:])
+            times_num(1, 1)
+            second = turn_out(second)
+            made = [turn_out(bank) for bank in late]
+            quantize(dz_mx[0], tokens, E5M2)
+            quantize(dzT_mx[0], first, E5M2)
+            quantize(dzT_mx[1], second, E5M2)
+            quantize_grad(1, 1, made)
+            held += [dy(1, 2, banks[0]), dy(1, 3, banks[6])]
+            for func in (ACT.Tanh, ACT.Square):
+                for jj in range(2):
+                    gate(1, jj, func)
+            prepare(wo_mx[1], wo_raw[1][:])
+
+            times_gate(1, 0)
+            times_gate(1, 1)
+            round_dz(1, 0, held[0])
+            round_dz(1, 1, held[1])
+            first = turn_dz(1, 0, 2, banks[3])
+            round_dz(1, 2, held[2])
+            round_dz(1, 3, held[3])
+            second = turn_dz(1, 2, 2, banks[4])
+            for jj in range(2):
+                gate(2, jj, ACT.Tanh)
+            gate(2, 0, ACT.Square)
+            first = turn_out(first)
+            gate(2, 1, ACT.Square)
+            second = turn_out(second)
+            wo_last = weave(wo_raw[3][:])
+            tokens = weave(dz_sb[1][:])
+            quantize(wo_mx[3], wo_last, E4M3)
+            quantize(dz_mx[1], tokens, E5M2)
+            held = [dy(2, j, banks[j]) for j in range(3)]
+            wq_first = weave(rows[0][:], on_scalar)
+            square_root_den(3, 0)
+            times_num(2, 0)
+            quantize(dzT_mx[2], first, E5M2)
+            times_gate(2, 0)
+            quantize(dzT_mx[3], second, E5M2)
+            emit(dw_pairs, dw_rows, 0, 0, outs(), SS)
+            emit(dw_pairs, dw_rows, 0, 1, outs(), SS)
+
+            round_dz(2, 0, held[0])
+            round_dz(2, 1, held[1])
+            held.append(dy(2, 3, banks[0]))
+            first = turn_dz(2, 0, 2, banks[3])
+            wq_next = weave(rows[1][:])
+            quantize(wq_mx[0], wq_first, E4M3)
+            quantize(wq_mx[1], wq_next, E4M3)
+            emit(dw_pairs, dw_rows, 0, 2, outs(), SS)
+            first = turn_out(first)
+            emit(dw_pairs, dw_rows, 0, 3, outs(), SS)
+            prepare_two(wq_mx[2], rows[2][:], wq_mx[3], rows[3][:])
+            quantize(dzT_mx[4], first, E5M2)
+            square_root_den(3, 1)
+            gate(3, 0, ACT.Tanh)
+            gate(3, 1, ACT.Tanh)
+            gate(3, 0, ACT.Square)
+            times_num(2, 1)
+            times_num(3, 0)
+            times_gate(2, 1)
+            emit(dq_pairs, dq_rows, 0, 0, outs(), SS)
+            emit(dq_pairs, dq_rows, 0, 1, outs(), SS)
+            later = [dy(3, 0, banks[1])]
+            times_gate(3, 0)
+            round_dz(2, 2, held[2])
+            round_dz(2, 3, held[3])
+            second = turn_dz(2, 2, 2, banks[4])
+            held = later + [dy(3, 1, banks[2]), dy(3, 2, banks[0])]
+            second = turn_out(second)
+            gate(3, 1, ACT.Square)
+            times_num(3, 1)
+
+            round_dz(3, 0, held[0])
+            round_dz(3, 1, held[1])
+            quantize(dzT_mx[5], second, E5M2)
+            first = turn_dz(3, 0, 2, banks[3])
+            held.append(dy(3, 3, banks[1]))
+            emit(dq_pairs, dq_rows, 0, 2, outs(), SS)
+            first = turn_out(first)
+            emit(dq_pairs, dq_rows, 0, 3, outs(), SS)
+            tokens = weave(dz_sb[0][:])
+            times_gate(3, 1)
+            quantize(dz_mx[2], tokens, E5M2)
+            quantize(dzT_mx[6], first, E5M2)
+            emit(dq_pairs, dq_rows, 1, 0, outs(), SS)
+            emit(dq_pairs, dq_rows, 1, 1, outs(), SS)
+            round_dz(3, 2, held[2])
+            round_dz(3, 3, held[3], 0, 2 * P)
+            first = turn_dz(3, 2, 1, banks[3])
+            tokens = weave(dz_sb[1][:, :, 0 : 2 * P])
+            round_dz(3, 3, held[3], 2 * P, PASS)
+            quantize(dz_mx[3], tokens, E5M2)
+            first = turn_out(first)
+            second = turn_dz(3, 3, 1, banks[4])
+            tokens = weave(dz_sb[1][:, :, 2 * P : PASS])
+            quantize(dzT_mx[7], first, E5M2)
+            emit(dw_pairs, dw_rows, 1, 0, [banks[2], banks[0]], SS)
+            second = turn_out(second)
+            quantize(dz_mx[3], tokens, E5M2, 2 * P)
+            quantize(dzT_mx[7], second, E5M2, P)
+            emit(dw_pairs, dw_rows, 1, 1, outs(), SV)
+            emit(dq_pairs, dq_rows, 1, 2, [banks[1], banks[3]], SV)
+            emit(dw_pairs, dw_rows, 1, 2, [banks[4], banks[2]], SV)
+            emit(dq_pairs, dq_rows, 1, 3, outs(), SV)
+            emit(dw_pairs, dw_rows, 1, 3, [banks[0], banks[1]], SV, split=True)

@@ -15,19 +15,21 @@ ALU = mybir.AluOpType
 P = 128
 PACK = 4
 PASS = P * PACK
+HALF = PASS // 2
 D = 1024
 FLOPS = 3 * 2 * D * D * D
 
 
 def tile_aftfull_pb_v_kernel(tc, q, num, den, Wq, Wo, zq, grad_out, out_0, out_1):
     nc = tc.nc
+    on_scalar, on_vector = nc.scalar.copy, nc.vector.tensor_copy
 
     def by_pass(x):
-        return x.rearrange("b t w -> (b t) w").rearrange("(g p j) w -> g p j w", g=2, j=PACK)
+        return x.rearrange("(g p j) w -> g p j w", g=2, j=PACK)
 
-    q_h, num_h, den_h, z_h, g_h, dq_h = (by_pass(x) for x in (q, num, den, zq, grad_out, out_0))
-    wq_h = Wq.rearrange("(g p j) w -> g p j w", g=2, j=PACK)
-    wo_h = Wo.rearrange("(g p j) w -> g p j w", g=2, j=PACK)
+    q_hbm, num_hbm, den_hbm, z_hbm, grad_hbm, dq_hbm = (
+        by_pass(x.rearrange("b t w -> (b t) w")) for x in (q, num, den, zq, grad_out, out_0))
+    wq_hbm, wo_hbm = by_pass(Wq), by_pass(Wo)
 
     with ExitStack() as ctx:
         sb = ctx.enter_context(tc.tile_pool(name="sb", bufs=1))
@@ -36,36 +38,33 @@ def tile_aftfull_pb_v_kernel(tc, q, num, den, Wq, Wo, zq, grad_out, out_0, out_1
         def tiles(name, n, shape, dtype):
             return [sb.tile(shape, dtype, name=name + str(i), align_bytes=64) for i in range(n)]
 
+        def operands(name, n, width):
+            return list(zip(tiles(name + "_codes", n, [P, width], U32), tiles(name + "_scales", n, [P, width], U8)))
+
         ident = sb.tile([P, P], F32, name="ident")
         warm = sb.tile([P, 1], F32, name="warm")
         den_sb = tiles("den", 4, [P, 2 * D], BF16)
         grad_sb = tiles("grad", 4, [P, 2 * D], BF16)
         num_sb = tiles("num", 4, [P, PACK, PASS], BF16)
         z_sb = tiles("z", 4, [P, PACK, PASS], F32)
-        fac = tiles("fac", 2, [P, PACK, D], F32)
+        factor = tiles("factor", 2, [P, PACK, D], F32)
         wo_raw = tiles("wo_raw", 4, [P, PACK, PASS], BF16)
         rows = tiles("rows", 4, [P, PACK, PASS], BF16)
+        dz_sb = tiles("dz", 2, [P, PACK, PASS], BF16)
         woven = tiles("woven", 3, [P, PASS * PACK], BF16)
         turned = tiles("turned", 5, [P, 2 * PASS], BF16)
-        dz_sb = tiles("dz", 2, [P, PACK, PASS], BF16)
-
-        def operand(name, n, width):
-            return list(zip(tiles(name + "_codes", n, [P, width], U32), tiles(name + "_scales", n, [P, width], U8)))
-
-        wo_mx = operand("wo", 4, PASS)
-        q_mx = operand("q", 4, PASS)
-        wq_mx = operand("wq", 4, PASS)
-        gT_mx = operand("gT", 8, 2 * P)
-        dzT_mx = operand("dzT", 8, 2 * P)
-        dz_mx = operand("dz", 4, PASS)
-        banks = [ps.tile([P, PASS], F32, name="bank" + str(i)) for i in range(8)]
-        dy_banks, turn_banks, out_banks = banks[0:3], banks[3:5], banks[5:8]
         staged = [t[:].bitcast(F32) for t in den_sb + grad_sb[0:2]]
-        count = {"woven": 0, "turned": 0, "dy": 0, "turn": 0, "out": 0, "staged": 0}
+        wo_mx = operands("wo", 4, PASS)
+        q_mx = operands("q", 4, PASS)
+        wq_mx = operands("wq", 4, PASS)
+        gradT_mx = operands("gradT", 8, 2 * P)
+        dzT_mx = operands("dzT", 8, 2 * P)
+        dz_mx = operands("dz", 4, PASS)
+        empty_banks = [ps.tile([P, PASS], F32, name="bank" + str(i)) for i in range(8)]
 
-        def take(kind, pool):
-            count[kind] = count[kind] + 1
-            return pool[(count[kind] - 1) % len(pool)]
+        def rotate(pool):
+            pool.append(pool.pop(0))
+            return pool[-1]
 
         def cols(c):
             return slice(c * PASS, (c + 1) * PASS)
@@ -73,11 +72,14 @@ def tile_aftfull_pb_v_kernel(tc, q, num, den, Wq, Wo, zq, grad_out, out_0, out_1
         def load(dst, src):
             nc.sync.dma_start(out=dst, in_=src)
 
-        def load_pair(dst, src, g, jj):
-            load(dst[2 * g + jj][:].rearrange("p (j w) -> p j w", j=2), src[g, :, 2 * jj : 2 * jj + 2, :])
+        def load_pair(dst, src, g, j0):
+            load(dst[2 * g + j0 // 2][:].rearrange("p (j w) -> p j w", j=2), src[g, :, j0 : j0 + 2, :])
 
-        def weave(src, copy=nc.vector.tensor_copy):
-            dst = take("woven", woven)[:, 0 : PACK * src.shape[2]]
+        def load_block(dst, src, g, c):
+            load(dst[:], src[g, :, :, cols(c)])
+
+        def weave(src, copy=on_vector):
+            dst = rotate(woven)[:, 0 : PACK * src.shape[2]]
             copy(
                 out=dst.rearrange("p (c i t) -> p c t i", i=4, t=PACK),
                 in_=src.rearrange("p t (c i) -> p c t i", i=4),
@@ -88,143 +90,128 @@ def tile_aftfull_pb_v_kernel(tc, q, num, den, Wq, Wo, zq, grad_out, out_0, out_1
             hi = lo + src.shape[1] // PACK
             nc.vector.quantize_mx(out=dst[0][:, lo:hi].bitcast(fmt), scales=dst[1][:, lo:hi], in_=src)
 
-        def prepare_two(dst_a, src_a, dst_b, src_b):
-            a, b = weave(src_a), weave(src_b)
-            quantize(dst_a, a, E4M3)
-            quantize(dst_b, b, E4M3)
-
-        def turn(halves, bank):
+        def turn(halves):
+            bank = empty_banks.pop(0)
             for h, words in enumerate(halves):
                 for u in range(2):
                     nc.tensor.transpose(bank[:, (2 * h + u) * P : (2 * h + u + 1) * P], words[:, u : 2 * P : 2], ident[:])
-            return bank[:, 0 : 2 * P * len(halves)]
+            return bank
 
-        def turn_out(bank, copy=nc.scalar.copy):
-            dst = take("turned", turned)[:, 0 : 2 * bank.shape[1]]
+        def turn_out(bank, copy=on_scalar):
+            dst = rotate(turned)[:]
             copy(
                 out=dst.bitcast(F32).rearrange("p (h r u) -> p h r u", r=P, u=2),
-                in_=bank.rearrange("p (h u r) -> p h r u", r=P, u=2),
+                in_=bank[:].rearrange("p (h u r) -> p h r u", r=P, u=2),
             )
+            empty_banks.append(bank)
             return dst
 
-        def turn_grad(g, j, bank):
+        def turn_grad(g, j):
             words = grad_sb[2 * g + j // 2][:, (j % 2) * D : (j % 2 + 1) * D].bitcast(F32)
-            return turn([words[:, 0 : 2 * P], words[:, 2 * P : 4 * P]], bank)
+            return turn([words[:, 0 : 2 * P], words[:, 2 * P : 4 * P]])
 
-        def turn_dz(i, j0, n, bank):
-            return turn([dz_sb[i % 2][:, j, :].bitcast(F32) for j in range(j0, j0 + n)], bank)
+        def turn_dz(i, j0):
+            return turn([dz_sb[i % 2][:, j, :].bitcast(F32) for j in (j0, j0 + 1)])
 
-        def fac_part(i, jj):
-            return fac[i % 2][:, 2 * jj : 2 * jj + 2, cols(i // 2)]
+        def factor_part(i, j0, n, lo, hi):
+            return factor[i % 2][:, j0 : j0 + n, i // 2 * PASS + lo : i // 2 * PASS + hi]
 
         def root_den(g, j0, n):
             src = den_sb[2 * g + j0 // 2][:, (j0 % 2) * D : (j0 % 2 + n) * D]
-            nc.scalar.activation(out=fac[g][:, j0 : j0 + n, :].rearrange("p j w -> p (j w)"), in_=src, func=ACT.Abs_reciprocal_sqrt)
+            dst = factor[g][:, j0 : j0 + n, :].rearrange("p j w -> p (j w)")
+            nc.scalar.activation(out=dst, in_=src, func=ACT.Abs_reciprocal_sqrt)
 
-        def square_root_den(i, jj):
-            nc.scalar.activation(out=fac_part(i, jj), in_=fac_part(i, jj), func=ACT.Square)
+        def square_root_den(i, j0):
+            part = factor_part(i, j0, 2, 0, PASS)
+            nc.scalar.activation(out=part, in_=part, func=ACT.Square)
 
-        def times_num(i, jj):
-            nc.vector.tensor_tensor(out=fac_part(i, jj), in0=fac_part(i, jj), in1=num_sb[i][:, 2 * jj : 2 * jj + 2, :], op=ALU.mult)
+        def tanh_z(i, j0):
+            part = z_sb[i][:, j0 : j0 + 2, :]
+            nc.scalar.activation(out=part, in_=part, func=ACT.Tanh, scale=0.5)
 
-        def gate(i, jj, func):
-            part = z_sb[i][:, 2 * jj : 2 * jj + 2, :]
-            nc.scalar.activation(out=part, in_=part, func=func, scale=0.5 if func == ACT.Tanh else 1.0)
+        def square_tanh(i, j0):
+            part = z_sb[i][:, j0 : j0 + 2, :]
+            nc.scalar.activation(out=part, in_=part, func=ACT.Square)
 
-        def times_gate(i, jj):
+        def times_num(i, j0, lo=0, hi=PASS):
+            part = factor_part(i, j0, 2, lo, hi)
+            nc.vector.tensor_tensor(out=part, in0=part, in1=num_sb[i][:, j0 : j0 + 2, lo:hi], op=ALU.mult)
+
+        def times_gate(i, j0, lo=0, hi=PASS):
+            part = factor_part(i, j0, 2, lo, hi)
             nc.vector.scalar_tensor_tensor(
-                out=fac_part(i, jj), in0=z_sb[i][:, 2 * jj : 2 * jj + 2, :], scalar=1.0, in1=fac_part(i, jj),
-                op0=ALU.subtract, op1=ALU.mult)
+                out=part, in0=z_sb[i][:, j0 : j0 + 2, lo:hi], scalar=1.0, in1=part, op0=ALU.subtract, op1=ALU.mult)
 
-        def product(bank, pairs, passes=(0, 1)):
+        def product(bank, pairs, passes):
             for k in passes:
                 lhs, at, rhs = pairs[k]
                 nc.tensor.matmul_mx(
                     out=bank[:], lhsT=lhs[0][:, at : at + P].bitcast(E5M2), lhsT_scale=lhs[1][:, at : at + P],
                     rhs=rhs[0][:].bitcast(E4M3), rhs_scale=rhs[1][:], start=(k == 0), stop=(k == 1))
 
-        def dy(i, j, bank):
-            product(bank, [(gT_mx[4 * (i % 2) + j], k * P, wo_mx[2 * k + i // 2]) for k in range(2)])
+        def dy(i, j):
+            bank = empty_banks.pop(0)
+            product(bank, [(gradT_mx[4 * (i % 2) + j], k * P, wo_mx[2 * k + i // 2]) for k in range(2)], (0, 1))
             return bank
 
         def round_dz(i, j, bank, lo=0, hi=PASS):
             nc.vector.scalar_tensor_tensor(
                 out=dz_sb[i % 2][:, j, lo:hi], in0=bank[:, lo:hi], scalar=-0.25,
-                in1=fac[i % 2][:, j, i // 2 * PASS + lo : i // 2 * PASS + hi], op0=ALU.mult, op1=ALU.mult)
+                in1=factor_part(i, j, 1, lo, hi)[:, 0, :], op0=ALU.mult, op1=ALU.mult)
+            if hi == PASS:
+                empty_banks.append(bank)
 
-        def dq_pairs(g, j, n):
-            return [(dzT_mx[2 * (2 * c + g) + j // 2], (j % 2) * P, wq_mx[2 * c + n]) for c in range(2)]
+        def dq_tile(g, j):
+            pairs = [[(dzT_mx[2 * (2 * c + g) + j // 2], (j % 2) * P, wq_mx[2 * c + n]) for c in range(2)] for n in range(2)]
+            return pairs, dq_hbm[g, :, j, :]
 
-        def dw_pairs(c, m, n):
-            return [(dz_mx[2 * c + g], m * P, q_mx[2 * g + n]) for g in range(2)]
+        def dw_tile(c, m):
+            pairs = [[(dz_mx[2 * c + g], m * P, q_mx[2 * g + n]) for g in range(2)] for n in range(2)]
+            return pairs, out_1[c * PASS + m * P : c * PASS + (m + 1) * P, :]
 
-        def dq_rows(g, j):
-            return dq_h[g, :, j, :]
-
-        def dw_rows(c, m):
-            return out_1[c * PASS + m * P : c * PASS + (m + 1) * P, :]
-
-        def begin(pairs_of, a, b, two):
+        def begin(tile):
+            opened = [empty_banks.pop(0) for n in range(2)]
             for n in range(2):
-                product(two[n], pairs_of(a, b, n), (0,))
+                product(opened[n], tile[0][n], (0,))
+            return opened
 
-        def emit(pairs_of, rows_of, a, b, two, copies, passes=(0, 1), split=False):
-            stage = take("staged", staged)
-            for n in range(2):
-                product(two[n], pairs_of(a, b, n), passes)
-                copies[n](out=stage[:, cols(n)], in_=two[n][:])
+        def emit(tile, second=on_scalar, opened=None, split=False):
+            pairs, hbm = tile
+            stage = rotate(staged)
+            for n, copy in enumerate((on_scalar, second)):
+                bank = opened[n] if opened else empty_banks.pop(0)
+                product(bank, pairs[n], (1,) if opened else (0, 1))
+                copy(out=stage[:, cols(n)], in_=bank[:])
+                empty_banks.append(bank)
                 if split:
-                    nc.sync.dma_start(out=rows_of(a, b)[:, cols(n)], in_=stage[:, cols(n)])
+                    nc.sync.dma_start(out=hbm[:, cols(n)], in_=stage[:, cols(n)])
             if not split:
-                nc.sync.dma_start(out=rows_of(a, b), in_=stage)
-
-        def load_quarter(i):
-            load(num_sb[i][:], num_h[i % 2, :, :, cols(i // 2)])
-            load(z_sb[i][:], z_h[i % 2, :, :, cols(i // 2)])
-
-        def quantize_grad(g, jj, made):
-            for h in range(2):
-                quantize(gT_mx[4 * g + 2 * jj + h], made[h], E5M2)
-
-        on_scalar, on_vector = nc.scalar.copy, nc.vector.tensor_copy
-        SS, SV = (on_scalar, on_scalar), (on_scalar, on_vector)
-
-        def prepare(dst, src, copy=on_vector):
-            quantize(dst, weave(src, copy), E4M3)
-
-        def load_z(i, jj):
-            load(z_sb[i][:, 2 * jj : 2 * jj + 2, :], z_h[i % 2, :, 2 * jj : 2 * jj + 2, cols(i // 2)])
-
-        def load_num(i):
-            load(num_sb[i][:], num_h[i % 2, :, :, cols(i // 2)])
-
-        def load_rows(src, g, n):
-            load(rows[2 * g + n][:], src[g, :, :, cols(n)])
+                nc.sync.dma_start(out=hbm, in_=stage)
 
         with tc.manual_schedule():
             for j in range(2):
-                load(den_sb[0][:, j * D : (j + 1) * D], den_h[0, :, j, :])
-                load(wo_raw[2 * j][:], wo_h[j, :, :, cols(0)])
-            load_rows(q_h, 0, 0)
-            load_pair(den_sb, den_h, 0, 1)
-            load_rows(q_h, 0, 1)
-            load_pair(grad_sb, g_h, 0, 0)
-            load_pair(den_sb, den_h, 1, 0)
-            load_pair(grad_sb, g_h, 0, 1)
-            load_rows(q_h, 1, 0)
-            load_pair(den_sb, den_h, 1, 1)
-            load_rows(q_h, 1, 1)
-            load_z(0, 0)
-            load_num(0)
-            load_z(0, 1)
-            load_pair(grad_sb, g_h, 1, 0)
-            load_num(1)
-            load_pair(grad_sb, g_h, 1, 1)
-            load(z_sb[1][:], z_h[1, :, :, cols(0)])
+                load(den_sb[0][:, j * D : (j + 1) * D], den_hbm[0, :, j, :])
+                load_block(wo_raw[2 * j], wo_hbm, j, 0)
+            load_block(rows[0], q_hbm, 0, 0)
+            load_pair(den_sb, den_hbm, 0, 2)
+            load_pair(grad_sb, grad_hbm, 0, 0)
+            load_block(rows[1], q_hbm, 0, 1)
+            load_pair(den_sb, den_hbm, 1, 0)
+            load_pair(grad_sb, grad_hbm, 0, 2)
+            load_pair(den_sb, den_hbm, 1, 2)
+            load_block(rows[2], q_hbm, 1, 0)
+            load(z_sb[0][:, 0:2, :], z_hbm[0, :, 0:2, cols(0)])
+            load_block(rows[3], q_hbm, 1, 1)
+            load_block(num_sb[0], num_hbm, 0, 0)
+            load(z_sb[0][:, 2:4, :], z_hbm[0, :, 2:4, cols(0)])
+            load_pair(grad_sb, grad_hbm, 1, 0)
+            load_block(num_sb[1], num_hbm, 1, 0)
+            load_pair(grad_sb, grad_hbm, 1, 2)
+            load_block(z_sb[1], z_hbm, 1, 0)
             for k in range(2):
-                load(wo_raw[2 * k + 1][:], wo_h[k, :, :, cols(1)])
-            load_num(2)
-            load(z_sb[2][:], z_h[0, :, :, cols(1)])
+                load_block(wo_raw[2 * k + 1], wo_hbm, k, 1)
+            load_block(num_sb[2], num_hbm, 0, 1)
+            load_block(z_sb[2], z_hbm, 0, 1)
 
             nc.vector.memset(warm[:], 1.0)
             nc.scalar.activation(out=warm[:], in_=warm[:], func=ACT.Abs_reciprocal_sqrt)
@@ -235,157 +222,163 @@ def tile_aftfull_pb_v_kernel(tc, q, num, den, Wq, Wo, zq, grad_out, out_0, out_1
             square_root_den(0, 0)
             square_root_den(2, 0)
             root_den(0, 2, 2)
-            square_root_den(0, 1)
-            square_root_den(2, 1)
+            square_root_den(0, 2)
             root_den(1, 0, 2)
             root_den(1, 2, 2)
-            gate(0, 0, ACT.Tanh)
-            gate(0, 0, ACT.Square)
-            gate(0, 1, ACT.Tanh)
-            gate(0, 1, ACT.Square)
+            tanh_z(0, 0)
+            square_tanh(0, 0)
+            tanh_z(0, 2)
+            square_root_den(2, 2)
+            square_tanh(0, 2)
 
-            prepare(wo_mx[0], wo_raw[0][:])
-            prepare_two(wo_mx[2], wo_raw[2][:], q_mx[0], rows[0][:])
-            prepare(q_mx[1], rows[1][:])
-            for jj in range(2):
-                made = [turn_out(turn_grad(0, 2 * jj + h, banks[3 + 2 * jj + h]), on_vector) for h in range(2)]
-                quantize_grad(0, jj, made)
-            prepare_two(q_mx[2], rows[2][:], q_mx[3], rows[3][:])
-            load_rows(wq_h, 0, 0)
-            load_rows(wq_h, 0, 1)
-            load(z_sb[3][:], z_h[1, :, :, cols(1)])
-            load_num(3)
-            load_rows(wq_h, 1, 0)
-            load_rows(wq_h, 1, 1)
+            quantize(wo_mx[0], weave(wo_raw[0][:]), E4M3)
+            pair = [weave(wo_raw[2][:]), weave(rows[0][:])]
+            quantize(wo_mx[2], pair[0], E4M3)
+            quantize(q_mx[0], pair[1], E4M3)
+            for j0 in (0, 2):
+                in_psum = [turn_grad(0, j) for j in (j0, j0 + 1)]
+                grads = [turn_out(in_psum[0], on_vector)]
+                q_woven = weave(rows[1 + j0 // 2][:])
+                grads.append(turn_out(in_psum[1], on_vector))
+                quantize(q_mx[1 + j0 // 2], q_woven, E4M3)
+                for h in range(2):
+                    quantize(gradT_mx[j0 + h], grads[h], E5M2)
+            q_woven = weave(rows[3][:])
+            load_block(rows[0], wq_hbm, 0, 0)
+            load_block(rows[1], wq_hbm, 0, 1)
+            load_block(z_sb[3], z_hbm, 1, 1)
+            load_block(num_sb[3], num_hbm, 1, 1)
+            load_block(rows[2], wq_hbm, 1, 0)
+            load_block(rows[3], wq_hbm, 1, 1)
             times_num(0, 0)
-            times_num(0, 1)
+            quantize(q_mx[3], q_woven, E4M3)
 
-            def outs():
-                return [take("out", out_banks), take("out", out_banks)]
-
-            held = [dy(0, j, banks[j]) for j in range(3)]
-            late = [turn_grad(1, j, banks[5 + j]) for j in range(2)]
+            held = [dy(0, j) for j in range(4)]
+            in_psum = [turn_grad(1, j) for j in range(4)]
             times_gate(0, 0)
+            times_num(0, 2)
             round_dz(0, 0, held[0])
             round_dz(0, 1, held[1])
-            held.append(dy(0, 3, banks[0]))
-            first = turn_dz(0, 0, 2, banks[3])
-            times_gate(0, 1)
-            made = [turn_out(bank) for bank in late]
-            late = [turn_grad(1, 2, banks[7])]
+            first = turn_dz(0, 0)
+            times_gate(0, 2)
+            grads = [turn_out(bank) for bank in in_psum[0:2]]
+            quantize(gradT_mx[4], grads[0], E5M2)
             round_dz(0, 2, held[2])
             round_dz(0, 3, held[3])
-            second = turn_dz(0, 2, 2, banks[4])
-            late.append(turn_grad(1, 3, banks[5]))
-            quantize_grad(1, 0, made)
+            second = turn_dz(0, 2)
+            quantize(gradT_mx[5], grads[1], E5M2)
             square_root_den(1, 0)
             first = turn_out(first)
-            square_root_den(1, 1)
-            held = [dy(1, j, banks[1 + j]) for j in range(2)]
+            square_root_den(1, 2)
+            held = [dy(1, j) for j in range(2)]
             times_num(1, 0)
-            tokens = weave(dz_sb[0][:])
-            times_num(1, 1)
+            dz_woven = weave(dz_sb[0][:])
+            times_num(1, 2)
             second = turn_out(second)
-            made = [turn_out(bank) for bank in late]
-            quantize(dz_mx[0], tokens, E5M2)
+            grads = [turn_out(bank) for bank in in_psum[2:4]]
+            quantize(dz_mx[0], dz_woven, E5M2)
             quantize(dzT_mx[0], first, E5M2)
             quantize(dzT_mx[1], second, E5M2)
-            quantize_grad(1, 1, made)
-            held += [dy(1, 2, banks[0]), dy(1, 3, banks[6])]
-            for func in (ACT.Tanh, ACT.Square):
-                for jj in range(2):
-                    gate(1, jj, func)
-            prepare(wo_mx[1], wo_raw[1][:])
+            for h in range(2):
+                quantize(gradT_mx[6 + h], grads[h], E5M2)
+            held.extend(dy(1, j) for j in (2, 3))
+            for step in (tanh_z, square_tanh):
+                for j0 in (0, 2):
+                    step(1, j0)
 
+            wo_first = weave(wo_raw[1][:])
             times_gate(1, 0)
-            times_gate(1, 1)
+            times_gate(1, 2)
+            wo_last = weave(wo_raw[3][:], on_scalar)
+            wq_first = weave(rows[0][:], on_scalar)
             round_dz(1, 0, held[0])
             round_dz(1, 1, held[1])
-            first = turn_dz(1, 0, 2, banks[3])
+            first = turn_dz(1, 0)
             round_dz(1, 2, held[2])
             round_dz(1, 3, held[3])
-            second = turn_dz(1, 2, 2, banks[4])
-            for jj in range(2):
-                gate(2, jj, ACT.Tanh)
-            gate(2, 0, ACT.Square)
-            first = turn_out(first)
-            gate(2, 1, ACT.Square)
-            second = turn_out(second)
-            wo_last = weave(wo_raw[3][:])
-            tokens = weave(dz_sb[1][:])
+            second = turn_dz(1, 2)
+            quantize(wo_mx[1], wo_first, E4M3)
+            dz_woven = weave(dz_sb[1][:])
             quantize(wo_mx[3], wo_last, E4M3)
-            quantize(dz_mx[1], tokens, E5M2)
-            held = [dy(2, j, banks[j]) for j in range(3)]
-            wq_first = weave(rows[0][:], on_scalar)
-            square_root_den(3, 0)
+            quantize(dz_mx[1], dz_woven, E5M2)
+            tanh_z(2, 0)
+            first = turn_out(first)
+            square_tanh(2, 0)
+            second = turn_out(second)
+            held = [dy(2, j) for j in range(2)]
+            emit(dw_tile(0, 0))
             times_num(2, 0)
-            quantize(dzT_mx[2], first, E5M2)
+            quantize(wq_mx[0], wq_first, E4M3)
             times_gate(2, 0)
+            quantize(dzT_mx[2], first, E5M2)
             quantize(dzT_mx[3], second, E5M2)
-            emit(dw_pairs, dw_rows, 0, 0, outs(), SS)
-            emit(dw_pairs, dw_rows, 0, 1, outs(), SS)
+            tanh_z(2, 2)
+            emit(dw_tile(0, 1))
+            square_tanh(2, 2)
 
             round_dz(2, 0, held[0])
             round_dz(2, 1, held[1])
-            held.append(dy(2, 3, banks[0]))
-            first = turn_dz(2, 0, 2, banks[3])
-            wq_next = weave(rows[1][:])
-            quantize(wq_mx[0], wq_first, E4M3)
-            quantize(wq_mx[1], wq_next, E4M3)
-            emit(dw_pairs, dw_rows, 0, 2, outs(), SS)
+            emit(dw_tile(0, 2))
+            first = turn_dz(2, 0)
+            held = [dy(2, 2), dy(2, 3)]
+            pair = [weave(rows[1][:]), weave(rows[2][:])]
+            quantize(wq_mx[1], pair[0], E4M3)
+            quantize(wq_mx[2], pair[1], E4M3)
             first = turn_out(first)
-            emit(dw_pairs, dw_rows, 0, 3, outs(), SS)
-            prepare_two(wq_mx[2], rows[2][:], wq_mx[3], rows[3][:])
+            square_root_den(3, 0)
+            emit(dw_tile(0, 3))
+            tanh_z(3, 0)
+            square_root_den(3, 2)
+            square_tanh(3, 0)
+            wq_last = weave(rows[3][:])
             quantize(dzT_mx[4], first, E5M2)
-            square_root_den(3, 1)
-            gate(3, 0, ACT.Tanh)
-            gate(3, 1, ACT.Tanh)
-            gate(3, 0, ACT.Square)
-            times_num(2, 1)
+            times_num(2, 2)
+            quantize(wq_mx[3], wq_last, E4M3)
+            times_gate(2, 2)
             times_num(3, 0)
-            times_gate(2, 1)
-            emit(dq_pairs, dq_rows, 0, 0, outs(), SS)
-            emit(dq_pairs, dq_rows, 0, 1, outs(), SS)
-            later = [dy(3, 0, banks[1])]
-            times_gate(3, 0)
-            round_dz(2, 2, held[2])
-            round_dz(2, 3, held[3])
-            second = turn_dz(2, 2, 2, banks[4])
-            held = later + [dy(3, 1, banks[2]), dy(3, 2, banks[0])]
+            held.extend(dy(3, j) for j in range(2))
+            emit(dq_tile(0, 0))
+            emit(dq_tile(0, 1))
+            round_dz(2, 2, held[0])
+            round_dz(2, 3, held[1])
+            second = turn_dz(2, 2)
+            held = held[2:4] + [dy(3, 2), dy(3, 3)]
             second = turn_out(second)
-            gate(3, 1, ACT.Square)
-            times_num(3, 1)
+            tanh_z(3, 2)
+            times_gate(3, 0)
+            times_num(3, 2, 0, HALF)
 
+            quantize(dzT_mx[5], second, E5M2)
             round_dz(3, 0, held[0])
             round_dz(3, 1, held[1])
-            quantize(dzT_mx[5], second, E5M2)
-            first = turn_dz(3, 0, 2, banks[3])
-            held.append(dy(3, 3, banks[1]))
-            emit(dq_pairs, dq_rows, 0, 2, outs(), SS)
+            emit(dq_tile(0, 2))
+            first = turn_dz(3, 0)
             first = turn_out(first)
-            emit(dq_pairs, dq_rows, 0, 3, outs(), SS)
-            tokens = weave(dz_sb[0][:])
-            times_gate(3, 1)
-            quantize(dz_mx[2], tokens, E5M2)
+            square_tanh(3, 2)
+            emit(dq_tile(0, 3))
+            dz_woven = weave(dz_sb[0][:])
+            times_num(3, 2, HALF, PASS)
             quantize(dzT_mx[6], first, E5M2)
-            emit(dq_pairs, dq_rows, 1, 0, outs(), SS)
-            emit(dq_pairs, dq_rows, 1, 1, outs(), SS)
-            round_dz(3, 2, held[2])
-            round_dz(3, 3, held[3], 0, 2 * P)
-            first = turn_dz(3, 2, 1, banks[3])
-            tokens = weave(dz_sb[1][:, :, 0 : 2 * P])
-            round_dz(3, 3, held[3], 2 * P, PASS)
-            quantize(dz_mx[3], tokens, E5M2)
-            first = turn_out(first)
-            second = turn_dz(3, 3, 1, banks[4])
-            tokens = weave(dz_sb[1][:, :, 2 * P : PASS])
-            quantize(dzT_mx[7], first, E5M2)
-            emit(dw_pairs, dw_rows, 1, 0, [banks[2], banks[0]], SS)
-            second = turn_out(second)
-            quantize(dz_mx[3], tokens, E5M2, 2 * P)
-            quantize(dzT_mx[7], second, E5M2, P)
-            emit(dw_pairs, dw_rows, 1, 1, outs(), SV)
-            emit(dq_pairs, dq_rows, 1, 2, [banks[1], banks[3]], SV)
-            emit(dw_pairs, dw_rows, 1, 2, [banks[4], banks[2]], SV)
-            emit(dq_pairs, dq_rows, 1, 3, outs(), SV)
-            emit(dw_pairs, dw_rows, 1, 3, [banks[0], banks[1]], SV, split=True)
+            quantize(dz_mx[2], dz_woven, E5M2)
+            times_gate(3, 2, 0, HALF)
+            times_gate(3, 2, HALF, PASS)
+            round_dz(3, 2, held[2], 0, HALF)
+            round_dz(3, 3, held[3], 0, HALF)
+            emit(dq_tile(1, 0))
+            emit(dq_tile(1, 1))
+            opened = [begin(dw_tile(1, m)) for m in range(2)]
+            round_dz(3, 2, held[2], HALF, PASS)
+            dz_woven = weave(dz_sb[1][:, :, 0:HALF])
+            round_dz(3, 3, held[3], HALF, PASS)
+            quantize(dz_mx[3], dz_woven, E5M2)
+            emit(dw_tile(1, 0), opened=opened[0])
+            second = turn_dz(3, 2)
+            emit(dw_tile(1, 1), opened=opened[1])
+            dz_woven = weave(dz_sb[1][:, :, HALF:PASS])
+            quantize(dz_mx[3], dz_woven, E5M2, HALF)
+            second = turn_out(second, on_vector)
+            quantize(dzT_mx[7], second, E5M2)
+            emit(dw_tile(1, 2), on_vector)
+            emit(dw_tile(1, 3), on_vector)
+            emit(dq_tile(1, 2), on_vector)
+            emit(dq_tile(1, 3), on_vector, split=True)

@@ -45,20 +45,21 @@ def tile_aftfull_pb_v_kernel(tc, q, num, den, Wq, Wo, zq, grad_out, out_0, out_1
         warm = sb.tile([P, 1], F32, name="warm")
         den_sb = tiles("den", 4, [P, 2 * D], BF16)
         grad_sb = tiles("grad", 4, [P, 2 * D], BF16)
-        num_sb = tiles("num", 4, [P, PACK, PASS], BF16)
+        num_sb = tiles("num", 4, [P, 2 * D], BF16)
         z_sb = tiles("z", 4, [P, PACK, PASS], F32)
         factor = tiles("factor", 2, [P, PACK, D], F32)
-        wo_raw = tiles("wo_raw", 4, [P, PACK, PASS], BF16)
-        rows = tiles("rows", 4, [P, PACK, PASS], BF16)
+        wo_raw = tiles("wo_raw", 2, [P, PACK, PASS], BF16)
+        rows = tiles("rows", 2, [P, PACK, D], BF16)
         dz_sb = tiles("dz", 2, [P, PACK, PASS], BF16)
         woven = tiles("woven", 3, [P, PASS * PACK], BF16)
-        turned = tiles("turned", 5, [P, 2 * PASS], BF16)
+        woven_pass = sb.tile([P, D * PACK], BF16, name="woven_pass", align_bytes=64)
+        turned = tiles("turned", 3, [P, 2, D], BF16)
         staged = [t[:].bitcast(F32) for t in den_sb + grad_sb[0:2]]
         wo_mx = operands("wo", 4, PASS)
-        q_mx = operands("q", 4, PASS)
-        wq_mx = operands("wq", 4, PASS)
-        gradT_mx = operands("gradT", 8, 2 * P)
-        dzT_mx = operands("dzT", 8, 2 * P)
+        q_mx = operands("q", 2, D)
+        wq_mx = operands("wq", 2, D)
+        gradT_mx = operands("gradT", 4, PASS)
+        dzT_mx = operands("dzT", 4, PASS)
         dz_mx = operands("dz", 4, PASS)
         empty_banks = [ps.tile([P, PASS], F32, name="bank" + str(i)) for i in range(8)]
 
@@ -79,7 +80,8 @@ def tile_aftfull_pb_v_kernel(tc, q, num, den, Wq, Wo, zq, grad_out, out_0, out_1
             load(dst[:], src[g, :, :, cols(c)])
 
         def weave(src, copy=on_vector):
-            dst = rotate(woven)[:, 0 : PACK * src.shape[2]]
+            width = PACK * src.shape[2]
+            dst = woven_pass[:] if width == PACK * D else rotate(woven)[:, 0:width]
             copy(
                 out=dst.rearrange("p (c i t) -> p c t i", i=4, t=PACK),
                 in_=src.rearrange("p t (c i) -> p c t i", i=4),
@@ -97,14 +99,15 @@ def tile_aftfull_pb_v_kernel(tc, q, num, den, Wq, Wo, zq, grad_out, out_0, out_1
                     nc.tensor.transpose(bank[:, (2 * h + u) * P : (2 * h + u + 1) * P], words[:, u : 2 * P : 2], ident[:])
             return bank
 
-        def turn_out(bank, copy=on_scalar):
-            dst = rotate(turned)[:]
+        def turn_out(bank, dst, copy=on_scalar):
             copy(
                 out=dst.bitcast(F32).rearrange("p (h r u) -> p h r u", r=P, u=2),
                 in_=bank[:].rearrange("p (h u r) -> p h r u", r=P, u=2),
             )
             empty_banks.append(bank)
-            return dst
+
+        def whole(tile):
+            return tile[:].rearrange("p h w -> p (h w)")
 
         def turn_grad(g, j):
             words = grad_sb[2 * g + j // 2][:, (j % 2) * D : (j % 2 + 1) * D].bitcast(F32)
@@ -135,7 +138,8 @@ def tile_aftfull_pb_v_kernel(tc, q, num, den, Wq, Wo, zq, grad_out, out_0, out_1
 
         def times_num(i, j0, lo=0, hi=PASS):
             part = factor_part(i, j0, 2, lo, hi)
-            nc.vector.tensor_tensor(out=part, in0=part, in1=num_sb[i][:, j0 : j0 + 2, lo:hi], op=ALU.mult)
+            both = num_sb[2 * (i % 2) + j0 // 2][:].rearrange("p (j w) -> p j w", j=2)
+            nc.vector.tensor_tensor(out=part, in0=part, in1=both[:, :, i // 2 * PASS + lo : i // 2 * PASS + hi], op=ALU.mult)
 
         def times_gate(i, j0, lo=0, hi=PASS):
             part = factor_part(i, j0, 2, lo, hi)
@@ -144,14 +148,14 @@ def tile_aftfull_pb_v_kernel(tc, q, num, den, Wq, Wo, zq, grad_out, out_0, out_1
 
         def product(bank, pairs, passes):
             for k in passes:
-                lhs, at, rhs = pairs[k]
+                lhs, at, rhs, n = pairs[k]
                 nc.tensor.matmul_mx(
                     out=bank[:], lhsT=lhs[0][:, at : at + P].bitcast(E5M2), lhsT_scale=lhs[1][:, at : at + P],
-                    rhs=rhs[0][:].bitcast(E4M3), rhs_scale=rhs[1][:], start=(k == 0), stop=(k == 1))
+                    rhs=rhs[0][:, cols(n)].bitcast(E4M3), rhs_scale=rhs[1][:, cols(n)], start=(k == 0), stop=(k == 1))
 
         def dy(i, j):
             bank = empty_banks.pop(0)
-            product(bank, [(gradT_mx[4 * (i % 2) + j], k * P, wo_mx[2 * k + i // 2]) for k in range(2)], (0, 1))
+            product(bank, [(gradT_mx[2 * (i % 2) + j // 2], (2 * (j % 2) + k) * P, wo_mx[2 * k + i // 2], 0) for k in range(2)], (0, 1))
             return bank
 
         def round_dz(i, j, bank, lo=0, hi=PASS):
@@ -162,11 +166,11 @@ def tile_aftfull_pb_v_kernel(tc, q, num, den, Wq, Wo, zq, grad_out, out_0, out_1
                 empty_banks.append(bank)
 
         def dq_tile(g, j):
-            pairs = [[(dzT_mx[2 * (2 * c + g) + j // 2], (j % 2) * P, wq_mx[2 * c + n]) for c in range(2)] for n in range(2)]
+            pairs = [[(dzT_mx[2 * c + g], j * P, wq_mx[c], n) for c in range(2)] for n in range(2)]
             return pairs, dq_hbm[g, :, j, :]
 
         def dw_tile(c, m):
-            pairs = [[(dz_mx[2 * c + g], m * P, q_mx[2 * g + n]) for g in range(2)] for n in range(2)]
+            pairs = [[(dz_mx[2 * c + g], m * P, q_mx[g], n) for g in range(2)] for n in range(2)]
             return pairs, out_1[c * PASS + m * P : c * PASS + (m + 1) * P, :]
 
         def begin(tile):
@@ -191,27 +195,23 @@ def tile_aftfull_pb_v_kernel(tc, q, num, den, Wq, Wo, zq, grad_out, out_0, out_1
         with tc.manual_schedule():
             for j in range(2):
                 load(den_sb[0][:, j * D : (j + 1) * D], den_hbm[0, :, j, :])
-                load_block(wo_raw[2 * j], wo_hbm, j, 0)
-            load_block(rows[0], q_hbm, 0, 0)
-            load_pair(den_sb, den_hbm, 0, 2)
+                load_block(wo_raw[j], wo_hbm, j, 0)
             load_pair(grad_sb, grad_hbm, 0, 0)
-            load_block(rows[1], q_hbm, 0, 1)
+            load_pair(den_sb, den_hbm, 0, 2)
+            load(rows[0][:], q_hbm[0])
             load_pair(den_sb, den_hbm, 1, 0)
             load_pair(grad_sb, grad_hbm, 0, 2)
             load_pair(den_sb, den_hbm, 1, 2)
-            load_block(rows[2], q_hbm, 1, 0)
+            load(rows[1][:], q_hbm[1])
             load(z_sb[0][:, 0:2, :], z_hbm[0, :, 0:2, cols(0)])
-            load_block(rows[3], q_hbm, 1, 1)
-            load_block(num_sb[0], num_hbm, 0, 0)
+            load_pair(num_sb, num_hbm, 0, 0)
             load(z_sb[0][:, 2:4, :], z_hbm[0, :, 2:4, cols(0)])
+            load_pair(num_sb, num_hbm, 0, 2)
             load_pair(grad_sb, grad_hbm, 1, 0)
-            load_block(num_sb[1], num_hbm, 1, 0)
+            load_pair(num_sb, num_hbm, 1, 0)
             load_pair(grad_sb, grad_hbm, 1, 2)
+            load_pair(num_sb, num_hbm, 1, 2)
             load_block(z_sb[1], z_hbm, 1, 0)
-            for k in range(2):
-                load_block(wo_raw[2 * k + 1], wo_hbm, k, 1)
-            load_block(num_sb[2], num_hbm, 0, 1)
-            load_block(z_sb[2], z_hbm, 0, 1)
 
             nc.vector.memset(warm[:], 1.0)
             nc.scalar.activation(out=warm[:], in_=warm[:], func=ACT.Abs_reciprocal_sqrt)
@@ -231,66 +231,70 @@ def tile_aftfull_pb_v_kernel(tc, q, num, den, Wq, Wo, zq, grad_out, out_0, out_1
             square_root_den(2, 2)
             square_tanh(0, 2)
 
-            quantize(wo_mx[0], weave(wo_raw[0][:]), E4M3)
-            pair = [weave(wo_raw[2][:]), weave(rows[0][:])]
-            quantize(wo_mx[2], pair[0], E4M3)
-            quantize(q_mx[0], pair[1], E4M3)
-            for j0 in (0, 2):
-                in_psum = [turn_grad(0, j) for j in (j0, j0 + 1)]
-                grads = [turn_out(in_psum[0], on_vector)]
-                q_woven = weave(rows[1 + j0 // 2][:])
-                grads.append(turn_out(in_psum[1], on_vector))
-                quantize(q_mx[1 + j0 // 2], q_woven, E4M3)
-                for h in range(2):
-                    quantize(gradT_mx[j0 + h], grads[h], E5M2)
-            q_woven = weave(rows[3][:])
-            load_block(rows[0], wq_hbm, 0, 0)
-            load_block(rows[1], wq_hbm, 0, 1)
+            for k in range(2):
+                quantize(wo_mx[2 * k], weave(wo_raw[k][:]), E4M3)
+            for k in range(2):
+                load_block(wo_raw[k], wo_hbm, k, 1)
+            load_block(z_sb[2], z_hbm, 0, 1)
+            grads = [rotate(turned), rotate(turned)]
+            in_psum = [turn_grad(0, j) for j in range(4)]
+            for j in (0, 1):
+                turn_out(in_psum[j], grads[0][:, j, :], on_vector)
+            q_woven = weave(rows[0][:])
+            quantize(gradT_mx[0], whole(grads[0]), E5M2)
+            quantize(q_mx[0], q_woven, E4M3)
+            for j in (2, 3):
+                turn_out(in_psum[j], grads[1][:, j - 2, :], on_vector)
+            q_woven = weave(rows[1][:])
+            load(rows[0][:], wq_hbm[0])
             load_block(z_sb[3], z_hbm, 1, 1)
-            load_block(num_sb[3], num_hbm, 1, 1)
-            load_block(rows[2], wq_hbm, 1, 0)
-            load_block(rows[3], wq_hbm, 1, 1)
+            load(rows[1][:], wq_hbm[1])
+            quantize(gradT_mx[1], whole(grads[1]), E5M2)
             times_num(0, 0)
-            quantize(q_mx[3], q_woven, E4M3)
+            quantize(q_mx[1], q_woven, E4M3)
 
             held = [dy(0, j) for j in range(4)]
-            in_psum = [turn_grad(1, j) for j in range(4)]
+            in_psum = [turn_grad(1, j) for j in range(2)]
             times_gate(0, 0)
             times_num(0, 2)
             round_dz(0, 0, held[0])
             round_dz(0, 1, held[1])
             first = turn_dz(0, 0)
+            in_psum.extend(turn_grad(1, j) for j in (2, 3))
             times_gate(0, 2)
-            grads = [turn_out(bank) for bank in in_psum[0:2]]
-            quantize(gradT_mx[4], grads[0], E5M2)
+            grads = rotate(turned)
+            for j in (0, 1):
+                turn_out(in_psum[j], grads[:, j, :])
+            quantize(gradT_mx[2], whole(grads), E5M2)
             round_dz(0, 2, held[2])
             round_dz(0, 3, held[3])
             second = turn_dz(0, 2)
-            quantize(gradT_mx[5], grads[1], E5M2)
             square_root_den(1, 0)
-            first = turn_out(first)
+            dz_turned = rotate(turned)
+            turn_out(first, dz_turned[:, 0, :])
             square_root_den(1, 2)
             held = [dy(1, j) for j in range(2)]
             times_num(1, 0)
             dz_woven = weave(dz_sb[0][:])
             times_num(1, 2)
-            second = turn_out(second)
-            grads = [turn_out(bank) for bank in in_psum[2:4]]
+            tanh_z(1, 0)
+            turn_out(second, dz_turned[:, 1, :])
+            grads = rotate(turned)
+            for j in (2, 3):
+                turn_out(in_psum[j], grads[:, j - 2, :])
             quantize(dz_mx[0], dz_woven, E5M2)
-            quantize(dzT_mx[0], first, E5M2)
-            quantize(dzT_mx[1], second, E5M2)
-            for h in range(2):
-                quantize(gradT_mx[6 + h], grads[h], E5M2)
+            quantize(dzT_mx[0], whole(dz_turned), E5M2)
+            quantize(gradT_mx[3], whole(grads), E5M2)
             held.extend(dy(1, j) for j in (2, 3))
-            for step in (tanh_z, square_tanh):
-                for j0 in (0, 2):
-                    step(1, j0)
+            tanh_z(1, 2)
+            for j0 in (0, 2):
+                square_tanh(1, j0)
 
-            wo_first = weave(wo_raw[1][:])
+            wo_first = weave(wo_raw[0][:])
             times_gate(1, 0)
             times_gate(1, 2)
-            wo_last = weave(wo_raw[3][:], on_scalar)
-            wq_first = weave(rows[0][:], on_scalar)
+            wo_last = weave(wo_raw[1][:], on_scalar)
+            wq_first = weave(rows[0][:, :, cols(0)], on_scalar)
             round_dz(1, 0, held[0])
             round_dz(1, 1, held[1])
             first = turn_dz(1, 0)
@@ -302,16 +306,17 @@ def tile_aftfull_pb_v_kernel(tc, q, num, den, Wq, Wo, zq, grad_out, out_0, out_1
             quantize(wo_mx[3], wo_last, E4M3)
             quantize(dz_mx[1], dz_woven, E5M2)
             tanh_z(2, 0)
-            first = turn_out(first)
+            dz_turned = rotate(turned)
+            turn_out(first, dz_turned[:, 0, :])
             square_tanh(2, 0)
-            second = turn_out(second)
+            turn_out(second, dz_turned[:, 1, :])
+            square_root_den(3, 0)
             held = [dy(2, j) for j in range(2)]
             emit(dw_tile(0, 0))
             times_num(2, 0)
             quantize(wq_mx[0], wq_first, E4M3)
             times_gate(2, 0)
-            quantize(dzT_mx[2], first, E5M2)
-            quantize(dzT_mx[3], second, E5M2)
+            quantize(dzT_mx[1], whole(dz_turned), E5M2)
             tanh_z(2, 2)
             emit(dw_tile(0, 1))
             square_tanh(2, 2)
@@ -321,19 +326,19 @@ def tile_aftfull_pb_v_kernel(tc, q, num, den, Wq, Wo, zq, grad_out, out_0, out_1
             emit(dw_tile(0, 2))
             first = turn_dz(2, 0)
             held = [dy(2, 2), dy(2, 3)]
-            pair = [weave(rows[1][:]), weave(rows[2][:])]
-            quantize(wq_mx[1], pair[0], E4M3)
-            quantize(wq_mx[2], pair[1], E4M3)
-            first = turn_out(first)
-            square_root_den(3, 0)
+            wq_second = weave(rows[0][:, :, cols(1)])
+            wq_last = weave(rows[1][:])
+            quantize(wq_mx[0], wq_second, E4M3, PASS)
+            dz_turned = rotate(turned)
+            turn_out(first, dz_turned[:, 0, :])
             emit(dw_tile(0, 3))
             tanh_z(3, 0)
             square_root_den(3, 2)
             square_tanh(3, 0)
-            wq_last = weave(rows[3][:])
-            quantize(dzT_mx[4], first, E5M2)
+            tanh_z(3, 2)
+            quantize(wq_mx[1], wq_last, E4M3)
             times_num(2, 2)
-            quantize(wq_mx[3], wq_last, E4M3)
+            quantize(dzT_mx[2], dz_turned[:, 0, :], E5M2)
             times_gate(2, 2)
             times_num(3, 0)
             held.extend(dy(3, j) for j in range(2))
@@ -343,42 +348,40 @@ def tile_aftfull_pb_v_kernel(tc, q, num, den, Wq, Wo, zq, grad_out, out_0, out_1
             round_dz(2, 3, held[1])
             second = turn_dz(2, 2)
             held = held[2:4] + [dy(3, 2), dy(3, 3)]
-            second = turn_out(second)
-            tanh_z(3, 2)
+            turn_out(second, dz_turned[:, 1, :])
+            square_tanh(3, 2)
             times_gate(3, 0)
             times_num(3, 2, 0, HALF)
 
-            quantize(dzT_mx[5], second, E5M2)
+            quantize(dzT_mx[2], dz_turned[:, 1, :], E5M2, HALF)
             round_dz(3, 0, held[0])
             round_dz(3, 1, held[1])
             emit(dq_tile(0, 2))
-            first = turn_dz(3, 0)
-            first = turn_out(first)
-            square_tanh(3, 2)
+            dz_turned = rotate(turned)
+            turn_out(turn_dz(3, 0), dz_turned[:, 0, :])
             emit(dq_tile(0, 3))
             dz_woven = weave(dz_sb[0][:])
-            times_num(3, 2, HALF, PASS)
-            quantize(dzT_mx[6], first, E5M2)
-            quantize(dz_mx[2], dz_woven, E5M2)
+            quantize(dzT_mx[3], dz_turned[:, 0, :], E5M2)
             times_gate(3, 2, 0, HALF)
-            times_gate(3, 2, HALF, PASS)
+            quantize(dz_mx[2], dz_woven, E5M2)
             round_dz(3, 2, held[2], 0, HALF)
             round_dz(3, 3, held[3], 0, HALF)
             emit(dq_tile(1, 0))
             emit(dq_tile(1, 1))
-            opened = [begin(dw_tile(1, m)) for m in range(2)]
-            round_dz(3, 2, held[2], HALF, PASS)
+            opened = [begin(tile) for tile in (dw_tile(1, 0), dw_tile(1, 1), dq_tile(1, 2))]
+            times_num(3, 2, HALF, PASS)
             dz_woven = weave(dz_sb[1][:, :, 0:HALF])
-            round_dz(3, 3, held[3], HALF, PASS)
+            times_gate(3, 2, HALF, PASS)
             quantize(dz_mx[3], dz_woven, E5M2)
-            emit(dw_tile(1, 0), opened=opened[0])
-            second = turn_dz(3, 2)
+            round_dz(3, 2, held[2], HALF, PASS)
+            round_dz(3, 3, held[3], HALF, PASS)
+            emit(dw_tile(1, 0), opened=opened[0], split=True)
             emit(dw_tile(1, 1), opened=opened[1])
-            dz_woven = weave(dz_sb[1][:, :, HALF:PASS])
-            quantize(dz_mx[3], dz_woven, E5M2, HALF)
-            second = turn_out(second, on_vector)
-            quantize(dzT_mx[7], second, E5M2)
-            emit(dw_tile(1, 2), on_vector)
+            second = turn_dz(3, 2)
+            quantize(dz_mx[3], weave(dz_sb[1][:, :, HALF:PASS]), E5M2, HALF)
+            turn_out(second, dz_turned[:, 1, :], on_vector)
+            quantize(dzT_mx[3], dz_turned[:, 1, :], E5M2, HALF)
+            emit(dw_tile(1, 2))
             emit(dw_tile(1, 3), on_vector)
-            emit(dq_tile(1, 2), on_vector)
+            emit(dq_tile(1, 2), on_vector, opened=opened[2])
             emit(dq_tile(1, 3), on_vector, split=True)

@@ -83,8 +83,8 @@ def tile_aftfull_pb_v_kernel(tc, q, num, den, Wq, Wo, zq, grad_out, out_0, out_1
             width = PACK * src.shape[2]
             dst = woven_pass[:] if width == PACK * D else rotate(woven)[:, 0:width]
             copy(
-                out=dst.rearrange("p (c i t) -> p c t i", i=4, t=PACK),
-                in_=src.rearrange("p t (c i) -> p c t i", i=4),
+                out=dst.rearrange("p (c i t) -> p c t i", i=2, t=PACK),
+                in_=src.rearrange("p t (c i) -> p c t i", i=2),
             )
             return dst
 

from contextlib import ExitStack

import concourse.mybir as mybir
from concourse.masks import make_identity

F32 = mybir.dt.float32
BF16 = mybir.dt.bfloat16
U32 = mybir.dt.uint32
U8 = mybir.dt.uint8
E4M3 = mybir.dt.float8_e4m3fn_x4
E5M2 = mybir.dt.float8_e5m2_x4
ACT = mybir.ActivationFunctionType
ALU = mybir.AluOpType

P = 128
PACK = 4
PASS = P * PACK
HALF = PASS // 2
D = 1024
FLOPS = 3 * 2 * D * D * D


def tile_aftfull_pb_v_kernel(tc, q, num, den, Wq, Wo, zq, grad_out, out_0, out_1):
    nc = tc.nc
    on_scalar, on_vector = nc.scalar.copy, nc.vector.tensor_copy

    def by_pass(x):
        return x.rearrange("(g p j) w -> g p j w", g=2, j=PACK)

    q_hbm, num_hbm, den_hbm, z_hbm, grad_hbm, dq_hbm = (
        by_pass(x.rearrange("b t w -> (b t) w")) for x in (q, num, den, zq, grad_out, out_0))
    wq_hbm, wo_hbm = by_pass(Wq), by_pass(Wo)

    with ExitStack() as ctx:
        sb = ctx.enter_context(tc.tile_pool(name="sb", bufs=1))
        ps = ctx.enter_context(tc.psum_pool(name="ps", bufs=1))

        def tiles(name, n, shape, dtype):
            return [sb.tile(shape, dtype, name=name + str(i), align_bytes=64) for i in range(n)]

        def operands(name, n, width):
            return list(zip(tiles(name + "_codes", n, [P, width], U32), tiles(name + "_scales", n, [P, width], U8)))

        ident = sb.tile([P, P], F32, name="ident")
        warm = sb.tile([P, 1], F32, name="warm")
        den_sb = tiles("den", 4, [P, 2 * D], BF16)
        grad_sb = tiles("grad", 4, [P, 2 * D], BF16)
        num_sb = tiles("num", 4, [P, 2 * D], BF16)
        z_sb = tiles("z", 4, [P, PACK, PASS], F32)
        factor = tiles("factor", 2, [P, PACK, D], F32)
        wo_raw = tiles("wo_raw", 2, [P, PACK, PASS], BF16)
        rows = tiles("rows", 2, [P, PACK, D], BF16)
        dz_sb = tiles("dz", 2, [P, PACK, PASS], BF16)
        woven = tiles("woven", 3, [P, PASS * PACK], BF16)
        woven_pass = sb.tile([P, D * PACK], BF16, name="woven_pass", align_bytes=64)
        turned = tiles("turned", 3, [P, 2, D], BF16)
        staged = [t[:].bitcast(F32) for t in den_sb + grad_sb[0:2]]
        wo_mx = operands("wo", 4, PASS)
        q_mx = operands("q", 2, D)
        wq_mx = operands("wq", 2, D)
        gradT_mx = operands("gradT", 4, PASS)
        dzT_mx = operands("dzT", 4, PASS)
        dz_mx = operands("dz", 4, PASS)
        empty_banks = [ps.tile([P, PASS], F32, name="bank" + str(i)) for i in range(8)]

        def rotate(pool):
            pool.append(pool.pop(0))
            return pool[-1]

        def cols(c):
            return slice(c * PASS, (c + 1) * PASS)

        def load(dst, src):
            nc.sync.dma_start(out=dst, in_=src)

        def load_pair(dst, src, g, j0):
            load(dst[2 * g + j0 // 2][:].rearrange("p (j w) -> p j w", j=2), src[g, :, j0 : j0 + 2, :])

        def load_block(dst, src, g, c):
            load(dst[:], src[g, :, :, cols(c)])

        def weave(src, copy=on_vector):
            width = PACK * src.shape[2]
            dst = woven_pass[:] if width == PACK * D else rotate(woven)[:, 0:width]
            copy(
                out=dst.rearrange("p (c i t) -> p c t i", i=2, t=PACK),
                in_=src.rearrange("p t (c i) -> p c t i", i=2),
            )
            return dst

        def quantize(dst, src, fmt, lo=0):
            hi = lo + src.shape[1] // PACK
            nc.vector.quantize_mx(out=dst[0][:, lo:hi].bitcast(fmt), scales=dst[1][:, lo:hi], in_=src)

        def turn(halves):
            bank = empty_banks.pop(0)
            for h, words in enumerate(halves):
                for u in range(2):
                    nc.tensor.transpose(bank[:, (2 * h + u) * P : (2 * h + u + 1) * P], words[:, u : 2 * P : 2], ident[:])
            return bank

        def turn_out(bank, dst, copy=on_scalar):
            copy(
                out=dst.bitcast(F32).rearrange("p (h r u) -> p h r u", r=P, u=2),
                in_=bank[:].rearrange("p (h u r) -> p h r u", r=P, u=2),
            )
            empty_banks.append(bank)

        def whole(tile):
            return tile[:].rearrange("p h w -> p (h w)")

        def turn_grad(g, j):
            words = grad_sb[2 * g + j // 2][:, (j % 2) * D : (j % 2 + 1) * D].bitcast(F32)
            return turn([words[:, 0 : 2 * P], words[:, 2 * P : 4 * P]])

        def turn_dz(i, j0):
            return turn([dz_sb[i % 2][:, j, :].bitcast(F32) for j in (j0, j0 + 1)])

        def factor_part(i, j0, n, lo, hi):
            return factor[i % 2][:, j0 : j0 + n, i // 2 * PASS + lo : i // 2 * PASS + hi]

        def root_den(g, j0, n):
            src = den_sb[2 * g + j0 // 2][:, (j0 % 2) * D : (j0 % 2 + n) * D]
            dst = factor[g][:, j0 : j0 + n, :].rearrange("p j w -> p (j w)")
            nc.scalar.activation(out=dst, in_=src, func=ACT.Abs_reciprocal_sqrt)

        def square_root_den(i, j0):
            part = factor_part(i, j0, 2, 0, PASS)
            nc.scalar.activation(out=part, in_=part, func=ACT.Square)

        def tanh_z(i, j0):
            part = z_sb[i][:, j0 : j0 + 2, :]
            nc.scalar.activation(out=part, in_=part, func=ACT.Tanh, scale=0.5)

        def square_tanh(i, j0):
            part = z_sb[i][:, j0 : j0 + 2, :]
            nc.scalar.activation(out=part, in_=part, func=ACT.Square)

        def times_num(i, j0, lo=0, hi=PASS):
            part = factor_part(i, j0, 2, lo, hi)
            both = num_sb[2 * (i % 2) + j0 // 2][:].rearrange("p (j w) -> p j w", j=2)
            nc.vector.tensor_tensor(out=part, in0=part, in1=both[:, :, i // 2 * PASS + lo : i // 2 * PASS + hi], op=ALU.mult)

        def times_gate(i, j0, lo=0, hi=PASS):
            part = factor_part(i, j0, 2, lo, hi)
            nc.vector.scalar_tensor_tensor(
                out=part, in0=z_sb[i][:, j0 : j0 + 2, lo:hi], scalar=1.0, in1=part, op0=ALU.subtract, op1=ALU.mult)

        def product(bank, pairs, passes):
            for k in passes:
                lhs, at, rhs, n = pairs[k]
                nc.tensor.matmul_mx(
                    out=bank[:], lhsT=lhs[0][:, at : at + P].bitcast(E5M2), lhsT_scale=lhs[1][:, at : at + P],
                    rhs=rhs[0][:, cols(n)].bitcast(E4M3), rhs_scale=rhs[1][:, cols(n)], start=(k == 0), stop=(k == 1))

        def dy(i, j):
            bank = empty_banks.pop(0)
            product(bank, [(gradT_mx[2 * (i % 2) + j // 2], (2 * (j % 2) + k) * P, wo_mx[2 * k + i // 2], 0) for k in range(2)], (0, 1))
            return bank

        def round_dz(i, j, bank, lo=0, hi=PASS):
            nc.vector.scalar_tensor_tensor(
                out=dz_sb[i % 2][:, j, lo:hi], in0=bank[:, lo:hi], scalar=-0.25,
                in1=factor_part(i, j, 1, lo, hi)[:, 0, :], op0=ALU.mult, op1=ALU.mult)
            if hi == PASS:
                empty_banks.append(bank)

        def dq_tile(g, j):
            pairs = [[(dzT_mx[2 * c + g], j * P, wq_mx[c], n) for c in range(2)] for n in range(2)]
            return pairs, dq_hbm[g, :, j, :]

        def dw_tile(c, m):
            pairs = [[(dz_mx[2 * c + g], m * P, q_mx[g], n) for g in range(2)] for n in range(2)]
            return pairs, out_1[c * PASS + m * P : c * PASS + (m + 1) * P, :]

        def begin(tile):
            opened = [empty_banks.pop(0) for n in range(2)]
            for n in range(2):
                product(opened[n], tile[0][n], (0,))
            return opened

        def emit(tile, second=on_scalar, opened=None, split=False):
            pairs, hbm = tile
            stage = rotate(staged)
            for n, copy in enumerate((on_scalar, second)):
                bank = opened[n] if opened else empty_banks.pop(0)
                product(bank, pairs[n], (1,) if opened else (0, 1))
                copy(out=stage[:, cols(n)], in_=bank[:])
                empty_banks.append(bank)
                if split:
                    nc.sync.dma_start(out=hbm[:, cols(n)], in_=stage[:, cols(n)])
            if not split:
                nc.sync.dma_start(out=hbm, in_=stage)

        with tc.manual_schedule():
            for j in range(2):
                load(den_sb[0][:, j * D : (j + 1) * D], den_hbm[0, :, j, :])
                load_block(wo_raw[j], wo_hbm, j, 0)
            load_pair(grad_sb, grad_hbm, 0, 0)
            load_pair(den_sb, den_hbm, 0, 2)
            load(rows[0][:], q_hbm[0])
            load_pair(den_sb, den_hbm, 1, 0)
            load_pair(grad_sb, grad_hbm, 0, 2)
            load_pair(den_sb, den_hbm, 1, 2)
            load(rows[1][:], q_hbm[1])
            load(z_sb[0][:, 0:2, :], z_hbm[0, :, 0:2, cols(0)])
            load_pair(num_sb, num_hbm, 0, 0)
            load(z_sb[0][:, 2:4, :], z_hbm[0, :, 2:4, cols(0)])
            load_pair(num_sb, num_hbm, 0, 2)
            load_pair(grad_sb, grad_hbm, 1, 0)
            load_pair(num_sb, num_hbm, 1, 0)
            load_pair(grad_sb, grad_hbm, 1, 2)
            load_pair(num_sb, num_hbm, 1, 2)
            load_block(z_sb[1], z_hbm, 1, 0)

            nc.vector.memset(warm[:], 1.0)
            nc.scalar.activation(out=warm[:], in_=warm[:], func=ACT.Abs_reciprocal_sqrt)
            make_identity(nc, ident[:])

            root_den(0, 0, 1)
            root_den(0, 1, 1)
            square_root_den(0, 0)
            square_root_den(2, 0)
            root_den(0, 2, 2)
            square_root_den(0, 2)
            root_den(1, 0, 2)
            root_den(1, 2, 2)
            tanh_z(0, 0)
            square_tanh(0, 0)
            tanh_z(0, 2)
            square_root_den(2, 2)
            square_tanh(0, 2)

            for k in range(2):
                quantize(wo_mx[2 * k], weave(wo_raw[k][:]), E4M3)
            for k in range(2):
                load_block(wo_raw[k], wo_hbm, k, 1)
            load_block(z_sb[2], z_hbm, 0, 1)
            grads = [rotate(turned), rotate(turned)]
            in_psum = [turn_grad(0, j) for j in range(4)]
            for j in (0, 1):
                turn_out(in_psum[j], grads[0][:, j, :], on_vector)
            q_woven = weave(rows[0][:])
            quantize(gradT_mx[0], whole(grads[0]), E5M2)
            quantize(q_mx[0], q_woven, E4M3)
            for j in (2, 3):
                turn_out(in_psum[j], grads[1][:, j - 2, :], on_vector)
            q_woven = weave(rows[1][:])
            load(rows[0][:], wq_hbm[0])
            load_block(z_sb[3], z_hbm, 1, 1)
            load(rows[1][:], wq_hbm[1])
            quantize(gradT_mx[1], whole(grads[1]), E5M2)
            times_num(0, 0)
            quantize(q_mx[1], q_woven, E4M3)

            held = [dy(0, j) for j in range(4)]
            in_psum = [turn_grad(1, j) for j in range(2)]
            times_gate(0, 0)
            times_num(0, 2)
            round_dz(0, 0, held[0])
            round_dz(0, 1, held[1])
            first = turn_dz(0, 0)
            in_psum.extend(turn_grad(1, j) for j in (2, 3))
            times_gate(0, 2)
            grads = rotate(turned)
            for j in (0, 1):
                turn_out(in_psum[j], grads[:, j, :])
            quantize(gradT_mx[2], whole(grads), E5M2)
            round_dz(0, 2, held[2])
            round_dz(0, 3, held[3])
            second = turn_dz(0, 2)
            square_root_den(1, 0)
            dz_turned = rotate(turned)
            turn_out(first, dz_turned[:, 0, :])
            square_root_den(1, 2)
            held = [dy(1, j) for j in range(2)]
            times_num(1, 0)
            dz_woven = weave(dz_sb[0][:])
            times_num(1, 2)
            tanh_z(1, 0)
            turn_out(second, dz_turned[:, 1, :])
            grads = rotate(turned)
            for j in (2, 3):
                turn_out(in_psum[j], grads[:, j - 2, :])
            quantize(dz_mx[0], dz_woven, E5M2)
            quantize(dzT_mx[0], whole(dz_turned), E5M2)
            quantize(gradT_mx[3], whole(grads), E5M2)
            held.extend(dy(1, j) for j in (2, 3))
            tanh_z(1, 2)
            for j0 in (0, 2):
                square_tanh(1, j0)

            wo_first = weave(wo_raw[0][:])
            times_gate(1, 0)
            times_gate(1, 2)
            wo_last = weave(wo_raw[1][:], on_scalar)
            wq_first = weave(rows[0][:, :, cols(0)], on_scalar)
            round_dz(1, 0, held[0])
            round_dz(1, 1, held[1])
            first = turn_dz(1, 0)
            round_dz(1, 2, held[2])
            round_dz(1, 3, held[3])
            second = turn_dz(1, 2)
            quantize(wo_mx[1], wo_first, E4M3)
            dz_woven = weave(dz_sb[1][:])
            quantize(wo_mx[3], wo_last, E4M3)
            quantize(dz_mx[1], dz_woven, E5M2)
            tanh_z(2, 0)
            dz_turned = rotate(turned)
            turn_out(first, dz_turned[:, 0, :])
            square_tanh(2, 0)
            turn_out(second, dz_turned[:, 1, :])
            square_root_den(3, 0)
            held = [dy(2, j) for j in range(2)]
            emit(dw_tile(0, 0))
            times_num(2, 0)
            quantize(wq_mx[0], wq_first, E4M3)
            times_gate(2, 0)
            quantize(dzT_mx[1], whole(dz_turned), E5M2)
            tanh_z(2, 2)
            emit(dw_tile(0, 1))
            square_tanh(2, 2)

            round_dz(2, 0, held[0])
            round_dz(2, 1, held[1])
            emit(dw_tile(0, 2))
            first = turn_dz(2, 0)
            held = [dy(2, 2), dy(2, 3)]
            wq_second = weave(rows[0][:, :, cols(1)])
            wq_last = weave(rows[1][:])
            quantize(wq_mx[0], wq_second, E4M3, PASS)
            dz_turned = rotate(turned)
            turn_out(first, dz_turned[:, 0, :])
            emit(dw_tile(0, 3))
            tanh_z(3, 0)
            square_root_den(3, 2)
            square_tanh(3, 0)
            tanh_z(3, 2)
            quantize(wq_mx[1], wq_last, E4M3)
            times_num(2, 2)
            quantize(dzT_mx[2], dz_turned[:, 0, :], E5M2)
            times_gate(2, 2)
            times_num(3, 0)
            held.extend(dy(3, j) for j in range(2))
            emit(dq_tile(0, 0))
            emit(dq_tile(0, 1))
            round_dz(2, 2, held[0])
            round_dz(2, 3, held[1])
            second = turn_dz(2, 2)
            held = held[2:4] + [dy(3, 2), dy(3, 3)]
            turn_out(second, dz_turned[:, 1, :])
            square_tanh(3, 2)
            times_gate(3, 0)
            times_num(3, 2, 0, HALF)

            quantize(dzT_mx[2], dz_turned[:, 1, :], E5M2, HALF)
            round_dz(3, 0, held[0])
            round_dz(3, 1, held[1])
            emit(dq_tile(0, 2))
            dz_turned = rotate(turned)
            turn_out(turn_dz(3, 0), dz_turned[:, 0, :])
            emit(dq_tile(0, 3))
            dz_woven = weave(dz_sb[0][:])
            quantize(dzT_mx[3], dz_turned[:, 0, :], E5M2)
            times_gate(3, 2, 0, HALF)
            quantize(dz_mx[2], dz_woven, E5M2)
            round_dz(3, 2, held[2], 0, HALF)
            round_dz(3, 3, held[3], 0, HALF)
            emit(dq_tile(1, 0))
            emit(dq_tile(1, 1))
            opened = [begin(tile) for tile in (dw_tile(1, 0), dw_tile(1, 1), dq_tile(1, 2))]
            times_num(3, 2, HALF, PASS)
            dz_woven = weave(dz_sb[1][:, :, 0:HALF])
            times_gate(3, 2, HALF, PASS)
            quantize(dz_mx[3], dz_woven, E5M2)
            round_dz(3, 2, held[2], HALF, PASS)
            round_dz(3, 3, held[3], HALF, PASS)
            emit(dw_tile(1, 0), opened=opened[0], split=True)
            emit(dw_tile(1, 1), opened=opened[1])
            second = turn_dz(3, 2)
            quantize(dz_mx[3], weave(dz_sb[1][:, :, HALF:PASS]), E5M2, HALF)
            turn_out(second, dz_turned[:, 1, :], on_vector)
            quantize(dzT_mx[3], dz_turned[:, 1, :], E5M2, HALF)
            emit(dw_tile(1, 2))
            emit(dw_tile(1, 3), on_vector)
            emit(dq_tile(1, 2), on_vector, opened=opened[2])
            emit(dq_tile(1, 3), on_vector, split=True)
